import numpy as np
import ml_dtypes


def mxq(x, axis, fmt="e4m3"):
    dtype, down = {"e4m3": (ml_dtypes.float8_e4m3fn, 7), "e5m2": (ml_dtypes.float8_e5m2, 14)}[fmt]
    v = np.moveaxis(np.asarray(x, np.float32).astype(ml_dtypes.bfloat16).astype(np.float64), axis, -1)
    blocks = v.reshape(v.shape[:-1] + (-1, 32))
    amax = np.abs(blocks).max(-1, keepdims=True)
    byte = np.maximum(np.where(amax > 0, np.frexp(amax)[1] - 1 + 127, 0) - down, 1)
    scale = np.exp2(byte - 127.0)
    codes = (blocks / scale).astype(np.float32).astype(dtype).astype(np.float64)
    return np.moveaxis((codes * scale).reshape(v.shape), -1, axis)


WIDE = False


def mx_kscale(k):
    if not WIDE:
        return np.ones(k)
    levels = np.array([30, -30])
    if k % 512:
        return np.exp2(np.random.permutation(np.resize(levels, k // 32))).repeat(32)
    a = np.empty((k // 512, 16))
    for p in range(k // 512):
        a[p, :8] = np.random.permutation(np.resize(levels, 8))
        for g in range(8):
            far = levels[np.abs(levels - a[p, g]) >= 10]
            a[p, g + 8] = far[np.random.randint(len(far))]
    return np.exp2(a.ravel()).repeat(32)


BF16 = ml_dtypes.bfloat16


def bf(x):
    return np.asarray(x, np.float32).astype(BF16)


def f64(x):
    return np.asarray(x).astype(np.float64)


E2M1 = np.array([0.0, 0.5, 1.0, 1.5, 2.0, 3.0, 4.0, 6.0, -0.0, -0.5, -1.0, -1.5, -2.0, -3.0, -4.0, -6.0])


def pack_weight(w, fmt):
    k, n = w.shape
    w = f64(bf(w)).reshape(k // 32, 32, n)
    amax = np.abs(w).max(1)
    if fmt == "e4m3":
        byte = np.frexp(amax)[1] - 1 + 127 - 7
    else:
        mant, ex = np.frexp(amax / 6.0)
        byte = np.where(mant > 0.5, ex, ex - 1) + 127
    byte = np.clip(np.where(amax > 0, byte, 1), 1, 254)
    scaled = (w * np.exp2(127.0 - byte)[:, None, :]).reshape(k, n).astype(np.float32)
    by_word = np.ascontiguousarray(scaled.reshape(k // 512, 128, 4, n).transpose(0, 1, 3, 2))
    if fmt == "e4m3":
        words = by_word.astype(ml_dtypes.float8_e4m3fn).view(np.uint8)
    else:
        c = by_word.astype(ml_dtypes.float4_e2m1fn).view(np.uint8) & 0xF
        words = c[..., 0::2] | (c[..., 1::2] << 4)
    return np.ascontiguousarray(words), np.ascontiguousarray(byte.astype(np.uint8).reshape(k // 512, 16, n))


def unpack_weight(words, scales, fmt):
    g, p, n, _ = words.shape
    if fmt == "e4m3":
        vals = np.ascontiguousarray(words).view(ml_dtypes.float8_e4m3fn).astype(np.float64)
    else:
        nib = np.empty((g, p, n, 4), np.uint8)
        nib[..., 0::2] = words & 0xF
        nib[..., 1::2] = words >> 4
        vals = E2M1[nib]
    vals = vals * np.repeat(np.exp2(scales.astype(np.float64) - 127.0), 8, axis=1)[..., None]
    return vals.transpose(0, 1, 3, 2).reshape(g * 512, n)

def pack4(w):
    words, scales = pack_weight(w, "e2m1")
    return words.reshape(words.shape[0], 128, -1), scales


def unpack4(words, scales):
    return unpack_weight(words.reshape(words.shape[0], 128, -1, 2), scales, "e2m1")


B, T, FS, H, HD = 1, 1024, 512, 12, 128
D = H * HD
EPS = 1e-6
ROPE_BASE = 10000.0


def rmsnorm(u, g):
    var = np.mean(u * u, axis=-1, keepdims=True)
    return u * (1.0 / np.sqrt(var + EPS)) * g


def rope(u, cos, sin):
    ur = u.reshape(B, T, H, HD // 2, 2)
    a, b = ur[..., 0], ur[..., 1]
    c = cos[None, :, None, :]
    s = sin[None, :, None, :]
    return np.stack([a * c - b * s, a * s + b * c], axis=-1).reshape(B, T, H, HD)


def setup_inputs():
    s = mx_kscale(D)
    inv = ROPE_BASE ** (-np.arange(HD // 2) / (HD // 2))
    ang = np.arange(T)[:, None] * inv[None, :]
    x = bf(np.random.standard_normal((B, T, D)) * s)
    words, scales = pack4(np.random.standard_normal((D, D)) / np.sqrt(D) / s[:, None])
    return {"x": x,
            "w_words": words,
            "w_scales": scales,
            "b": bf(np.random.standard_normal(D) * 0.1),
            "g": bf(1.0 + 0.1 * np.random.standard_normal(D)),
            "freqs_cos": bf(np.cos(ang)),
            "freqs_sin": bf(np.sin(ang))}


def reference(x, w_words, w_scales, b, g, freqs_cos, freqs_sin):
    u = (mxq(f64(x), 2, "e5m2") @ unpack4(w_words, w_scales)) + f64(b)
    return rope(rmsnorm(u, f64(g)).reshape(B, T, H, HD), f64(freqs_cos), f64(freqs_sin))

@@ -1,0 +1,386 @@
+from contextlib import ExitStack
+
+import concourse.mybir as mybir
+from concourse.masks import make_identity
+
+T, D, HEADS, HD = 1024, 1536, 12, 128
+EPS = 1e-6
+FLOPS = 2 * T * D * D
+
+F32 = mybir.dt.float32
+BF16 = mybir.dt.bfloat16
+I32 = mybir.dt.int32
+U32 = mybir.dt.uint32
+U8 = mybir.dt.uint8
+E5M2X4 = mybir.dt.float8_e5m2_x4
+E2M1X4 = mybir.dt.float4_e2m1fn_x4
+ALU = mybir.AluOpType
+ACT = mybir.ActivationFunctionType
+
+P = 128
+TILES = T // P
+K_PASS = 512
+PASSES = D // K_PASS
+BANK = 512
+QUAD = 4
+QUADS = HEADS // QUAD
+PAIR = 2
+GAIN_ROW = 32
+GROUP_TILES = (2, 2, 2, 1, 1)
+HEAD_CHUNKS = 4
+BANKS_PER_STEP = 2
+EARLY_STEPS = 3
+FOLD_STEPS = 2
+GADD = True
+ORDER = 0
+VT_BUFS = 3
+EARLY_HEADS = 4
+FOLD2 = False
+LATE_FROM = 5
+SCALES = 1
+XT = 1
+VADDS = 1
+SPLIT_FROM = 5
+SPLITS = 2
+TABLE_STEP = 2
+
+
+def tile_causalwanmodel_pa_kernel(tc, x, w_words, w_scales, b, g, freqs_cos, freqs_sin, out):
+    nc = tc.nc
+    x_rows = x.rearrange("o (p n) d -> p (o n) d", n=TILES)
+    out_rows = out.rearrange("o (p n) h c -> p (o n) (h c)", n=TILES)
+
+    with ExitStack() as ctx:
+        keep = ctx.enter_context(tc.tile_pool(name="keep", bufs=1))
+        work = ctx.enter_context(tc.tile_pool(name="work", bufs=3))
+        psum = ctx.enter_context(tc.psum_pool(name="psum", bufs=1))
+        ctx.enter_context(tc.manual_schedule())
+
+        rows_bf = keep.tile([P, P], BF16, name="rows_bf")
+        nc.vector.memset(rows_bf[:], 0.0)
+        ident = keep.tile([P, P], F32, name="ident")
+        make_identity(nc, ident[:])
+
+        x_raw = {}
+
+        def load_x_pass(k):
+            t = keep.tile([P, PAIR, K_PASS], BF16, name="x_first%d" % k)
+            nc.sync.dma_start(out=t[:], in_=x_rows[:, 0:PAIR, K_PASS * k : K_PASS * (k + 1)])
+            x_raw[0, k] = t[:]
+
+        def load_x_pair(pair):
+            t = keep.tile([P, PAIR, D], BF16, name="x_pair%d" % pair)
+            nc.sync.dma_start(out=t[:], in_=x_rows[:, PAIR * pair : PAIR * (pair + 1), :])
+            for k in range(PASSES):
+                x_raw[pair, k] = t[:, :, K_PASS * k : K_PASS * (k + 1)]
+
+        w_codes = {}
+
+        def load_w(quad):
+            width = 2 * QUAD * HD
+            t = keep.tile([P, PASSES, width], U8, name="w_codes%d" % quad, align_bytes=64)
+            src = w_words[:, :, width * quad : width * (quad + 1)].rearrange("k p n -> p k n")
+            nc.sync.dma_start(out=t[:].bitcast(I32), in_=src.bitcast(I32))
+            w_codes[quad] = t
+
+        for k in range(PASSES):
+            load_x_pass(k)
+        w_plane = keep.tile([P, PASSES, D], U8, name="w_plane", align_bytes=64)
+        for q in range(4):
+            src = w_scales[:, 4 * q : 4 * q + 4, :].rearrange("k r n -> r k n")
+            nc.sync.dma_start(out=w_plane[32 * q : 32 * q + 4, :, :].bitcast(I32), in_=src.bitcast(I32))
+        load_w(0)
+        nc.sync.dma_start(out=rows_bf[0:HEADS, :], in_=b.rearrange("(h c) -> h c", c=HD))
+        nc.sync.dma_start(out=rows_bf[GAIN_ROW : GAIN_ROW + HEADS, :], in_=g.rearrange("(h c) -> h c", c=HD))
+        load_x_pair(1)
+        load_w(1)
+        load_w(2)
+        load_x_pair(2)
+        cos_bf = keep.tile([P, TILES * HD // 2], BF16, name="cos_bf")
+        sin_bf = keep.tile([P, TILES * HD // 2], BF16, name="sin_bf")
+        nc.sync.dma_start(out=cos_bf[:], in_=freqs_cos.rearrange("(p n) j -> p (n j)", n=TILES))
+        nc.sync.dma_start(out=sin_bf[:], in_=freqs_sin.rearrange("(p n) j -> p (n j)", n=TILES))
+        load_x_pair(3)
+
+        x_codes, x_plane, x_banks, x_grouped = {}, {}, {}, {}
+
+        def x_transpose(chunk, tag, bufs):
+            bank = psum.tile([P, 2, PAIR, P], F32, name="x_bank", tag=tag, bufs=bufs)
+            for n in range(PAIR):
+                words = x_raw[chunk][:, n, :].bitcast(F32)
+                for u in range(2):
+                    src = x_split[chunk][:, n, u, :] if chunk in x_split else words[:, u : K_PASS // 2 : 2]
+                    nc.tensor.transpose(bank[:, u, n, :], src, ident[:])
+            x_banks[chunk] = bank
+
+        x_split = {}
+
+        def x_deinterleave(chunk):
+            t = keep.tile([P, PAIR, 2, P], F32, name="x_split%d_%d" % chunk)
+            nc.vector.tensor_copy(out=t[:], in_=x_raw[chunk].bitcast(F32).rearrange("p n (m u) -> p n u m", u=2))
+            x_split[chunk] = t
+
+        def x_copy(chunk):
+            t = work.tile([P, PAIR * P * 4], BF16, name="x_grouped", align_bytes=64)
+            nc.scalar.copy(
+                out=t[:].bitcast(F32).rearrange("p (r u) -> p r u", u=2),
+                in_=x_banks[chunk][:].rearrange("p u n r -> p (n r) u"),
+            )
+            x_grouped[chunk] = t
+
+        def x_quantize(chunk):
+            codes = keep.tile([P, PAIR * P], U32, name="x_codes%d_%d" % chunk, align_bytes=64)
+            plane = keep.tile([P, PAIR * P], U8, name="x_plane%d_%d" % chunk, align_bytes=64)
+            nc.vector.quantize_mx(out=codes[:].bitcast(E5M2X4), scales=plane[:], in_=x_grouped[chunk][:])
+            x_codes[chunk], x_plane[chunk] = codes, plane
+
+        chunks = [(pair, k) for pair in range(TILES // PAIR) for k in range(PASSES)]
+
+        for chunk in chunks[:PASSES]:
+            x_transpose(chunk, "vt", VT_BUFS)
+            x_copy(chunk)
+        for chunk in chunks[:2]:
+            x_quantize(chunk)
+        rows_f32 = keep.tile([P, P], F32, name="rows_f32")
+        nc.vector.tensor_copy(out=rows_f32[:], in_=rows_bf[:])
+        cols_bank = psum.tile([P, P], F32, name="cols_bank", tag="ss", bufs=1)
+        nc.tensor.transpose(cols_bank[:], rows_f32[:], ident[:])
+        for chunk in chunks[2:PASSES]:
+            x_quantize(chunk)
+        cols = keep.tile([P, 2 * GAIN_ROW], F32, name="cols")
+        nc.vector.tensor_copy(out=cols[:], in_=cols_bank[:, 0 : 2 * GAIN_ROW])
+        gain_bias = keep.tile([P, HEADS], F32, name="gain_bias")
+        nc.vector.tensor_tensor(
+            out=gain_bias[:], in0=cols[:, 0:HEADS], in1=cols[:, GAIN_ROW : GAIN_ROW + HEADS], op=ALU.mult
+        )
+
+        cos2 = keep.tile([P, TILES, HD // 2, 2], F32, name="cos2")
+        sin2 = keep.tile([P, TILES, HD // 2, 2], F32, name="sin2")
+        sign = keep.tile([P, 1, 2], F32, name="sign")
+        nc.vector.memset(sign[:, :, 0:1], -1.0)
+        nc.vector.memset(sign[:, :, 1:2], 1.0)
+
+        def make_tables():
+            shape = [P, TILES * HD // 2, 2]
+            nc.scalar.copy(
+                out=cos2[:].rearrange("p n j e -> p (n j) e"),
+                in_=cos_bf[:].rearrange("p (m o) -> p m o", o=1).to_broadcast(shape),
+            )
+            nc.vector.tensor_tensor(
+                out=sin2[:].rearrange("p n j e -> p (n j) e"),
+                in0=sin_bf[:].rearrange("p (m o) -> p m o", o=1).to_broadcast(shape),
+                in1=sign[:].to_broadcast(shape),
+                op=ALU.mult,
+            )
+
+        first_tile = [sum(GROUP_TILES[:i]) for i in range(len(GROUP_TILES))]
+        steps = [(grp, quad) for grp in range(len(GROUP_TILES)) for quad in range(QUADS)]
+        mx_banks, gained, squares, folded, sum_bank, root, rstd, vt_banks = {}, {}, {}, {}, {}, {}, {}, {}
+
+        def multiply(step):
+            grp, quad = step
+            n = GROUP_TILES[grp] * P
+            pair, offset = divmod(first_tile[grp], PAIR)
+            tokens = slice(offset * P, offset * P + n)
+            per_bank = BANK // n
+            for i in range(QUAD):
+                if i % per_bank == 0:
+                    bank = psum.tile([P, per_bank, n], F32, name="mx_bank", tag="mx", bufs=7 - XT - VT_BUFS)
+                head = QUAD * quad + i
+                for k in range(PASSES):
+                    nc.tensor.matmul_mx(
+                        out=bank[:, i % per_bank, :],
+                        lhsT=w_codes[quad][:, k, 2 * HD * i : 2 * HD * (i + 1)].bitcast(E2M1X4),
+                        lhsT_scale=w_plane[:, k, HD * head : HD * (head + 1)],
+                        rhs=x_codes[pair, k][:, tokens].bitcast(E5M2X4),
+                        rhs_scale=x_plane[pair, k][:, tokens],
+                        start=(k == 0),
+                        stop=(k == PASSES - 1),
+                    )
+                mx_banks[step, i] = bank[:, i % per_bank, :]
+
+        def evacuate(step, gain_on_vector):
+            grp, quad = step
+            n = GROUP_TILES[grp] * P
+            per_bank = BANK // n
+            squares[step] = work.tile([P, QUAD, n], F32, name="squares", bufs=2)
+            gained[step] = work.tile([P, QUAD, n], F32, name="gained", bufs=7)
+            for i0 in range(0, QUAD, per_bank):
+                for i in range(i0, i0 + per_bank):
+                    head = QUAD * quad + i
+                    nc.scalar.activation(
+                        out=squares[step][:, i, :],
+                        in_=mx_banks[step, i],
+                        func=ACT.Square,
+                        bias=cols[:, head : head + 1],
+                    )
+                for i in range(i0, i0 + per_bank):
+                    head = QUAD * quad + i
+                    gain = cols[:, GAIN_ROW + head : GAIN_ROW + head + 1]
+                    if i >= QUAD - gain_on_vector:
+                        nc.vector.tensor_scalar(
+                            out=gained[step][:, i, :],
+                            in0=mx_banks[step, i],
+                            scalar1=gain,
+                            scalar2=gain_bias[:, head : head + 1],
+                            op0=ALU.mult,
+                            op1=ALU.add,
+                        )
+                    else:
+                        nc.scalar.activation(
+                            out=gained[step][:, i, :],
+                            in_=mx_banks[step, i],
+                            func=ACT.Identity,
+                            bias=gain_bias[:, head : head + 1],
+                            scale=gain,
+                        )
+
+        def fold(step):
+            n = GROUP_TILES[step[0]] * P
+            if steps.index(step) >= FOLD_STEPS:
+                folded[step] = squares[step]
+                return
+            folded[step] = work.tile([P, QUAD // 2, n], F32, name="folded", bufs=2)
+            nc.vector.tensor_tensor(
+                out=folded[step][:],
+                in0=squares[step][:, : QUAD // 2, :],
+                in1=squares[step][:, QUAD // 2 :, :],
+                op=ALU.add,
+            )
+            if FOLD2:
+                twice = work.tile([P, 1, n], F32, name="twice", bufs=2)
+                nc.vector.tensor_tensor(out=twice[:], in0=folded[step][:, 0:1, :], in1=folded[step][:, 1:2, :], op=ALU.add)
+                folded[step] = twice
+
+        def sum_transpose(step):
+            grp, quad = step
+            tiles = GROUP_TILES[grp]
+            if quad == 0:
+                sum_bank[grp] = psum.tile([P, tiles, P], F32, name="sum_bank", tag="ss", bufs=1)
+            parts = [(i, n) for i in range(folded[step].shape[1]) for n in range(tiles)]
+            for i, n in parts:
+                nc.tensor.matmul(
+                    out=sum_bank[grp][:, n, :],
+                    lhsT=folded[step][:, i, P * n : P * (n + 1)],
+                    rhs=ident[:],
+                    start=(quad == 0 and (i, n) == parts[0]),
+                    stop=(quad == QUADS - 1 and (i, n) == parts[-1]),
+                    is_transpose=True,
+                )
+
+        def norm_root(grp):
+            tiles = GROUP_TILES[grp]
+            total = work.tile([P, tiles], F32, name="total")
+            for n in range(tiles):
+                spent = work.tile([P, P], F32, name="spent")
+                nc.scalar.activation(
+                    out=spent[:], in_=sum_bank[grp][:, n, :], func=ACT.Identity, accum_out=total[:, n : n + 1]
+                )
+            root[grp] = work.tile([P, tiles], F32, name="root")
+            nc.scalar.activation(
+                out=root[grp][:], in_=total[:], func=ACT.Abs_reciprocal_sqrt, bias=EPS, scale=1.0 / D
+            )
+
+        def norm_reciprocal(grp):
+            rstd[grp] = root[grp]
+
+        def value_transpose(item):
+            grp, n, quad = item
+            bank = psum.tile([P, QUAD, HD // 2, 2], F32, name="vt_bank", tag="vt", bufs=VT_BUFS)
+            for i in range(QUAD):
+                nc.tensor.transpose(
+                    bank[:, i, :, :].rearrange("p j e -> p (j e)"),
+                    gained[grp, quad][:, i, P * n : P * (n + 1)],
+                    ident[:],
+                )
+            vt_banks[item] = bank
+
+        def rotate(item):
+            grp, n, quad = item
+            tile = first_tile[grp] + n
+            shape = [P, QUAD, HD // 2, 2]
+            bank = vt_banks[item]
+            by_cos = work.tile(shape, F32, name="by_cos")
+            by_sin = work.tile(shape, F32, name="by_sin")
+            for dst, src, table in ((by_cos, bank[:], cos2), (by_sin, bank[:, :, :, ::-1], sin2)):
+                factor = table[:, tile : tile + 1, :, :].to_broadcast(shape)
+                if grp in rstd:
+                    nc.vector.scalar_tensor_tensor(
+                        out=dst[:], in0=src, scalar=rstd[grp][:, n : n + 1], in1=factor, op0=ALU.mult, op1=ALU.mult
+                    )
+                else:
+                    nc.vector.tensor_tensor(out=dst[:], in0=src, in1=factor, op=ALU.mult)
+            result = work.tile([P, BANK], F32, name="result", bufs=10)
+            adder = nc.vector if item in vector_adds or not GADD else nc.gpsimd
+            adder.tensor_tensor(
+                out=result[:],
+                in0=by_cos[:].rearrange("p i j e -> p (i j e)"),
+                in1=by_sin[:].rearrange("p i j e -> p (i j e)"),
+                op=ALU.add,
+            )
+            if grp in rstd:
+                store(item, result)
+            else:
+                unscaled.append((item, result))
+
+        def store(item, result):
+            grp, n, quad = item
+            nc.sync.dma_start(out=out_rows[:, first_tile[grp] + n, BANK * quad : BANK * (quad + 1)], in_=result[:])
+
+        def scale_late(most):
+            for item, result in [entry for entry in unscaled if entry[0][0] in rstd][:most]:
+                grp, n, quad = item
+                unscaled.remove((item, result))
+                scaled = work.tile([P, BANK], F32, name="scaled", bufs=4)
+                nc.scalar.activation(out=scaled[:], in_=result[:], func=ACT.Copy, scale=rstd[grp][:, n : n + 1])
+                store(item, scaled)
+
+        unscaled = []
+        last_group = len(GROUP_TILES) - 1
+        vector_adds = [(last_group, n, QUADS - 1) for n in range(GROUP_TILES[last_group])][-VADDS:] if VADDS else []
+        copied = []
+        waiting = []
+        transposed = []
+        s = 0
+        while s <= len(steps) or waiting or transposed or unscaled:
+            step = steps[s] if s < len(steps) else None
+            before = steps[s - 1] if 1 <= s <= len(steps) else None
+            twice_before = steps[s - 2] if 2 <= s <= len(steps) + 1 else None
+            turned = chunks[PASSES + s + 1 : PASSES + s + 2] if s else chunks[PASSES : PASSES + 2]
+            if step:
+                multiply(step)
+            if before:
+                fold(before)
+            if twice_before and twice_before[1] == QUADS - 1:
+                norm_reciprocal(twice_before[0])
+            for item in transposed[:1]:
+                rotate(item)
+            for chunk in copied:
+                x_quantize(chunk)
+            for item in transposed[1:]:
+                rotate(item)
+            if step:
+                evacuate(step, EARLY_HEADS if s < EARLY_STEPS else 0)
+            scale_late(SCALES if step else 99)
+            for chunk in chunks[max(SPLIT_FROM, 2 * s + 4) : 2 * s + 6]:
+                x_deinterleave(chunk)
+            if s == TABLE_STEP:
+                make_tables()
+            if before:
+                sum_transpose(before)
+            for chunk in turned:
+                x_transpose(chunk, *(("xt", 1) if s and XT else ("vt", VT_BUFS)))
+            if before and before[0] >= LATE_FROM:
+                waiting.extend((before[0], n, before[1]) for n in range(GROUP_TILES[before[0]]))
+            elif before and before[1] == QUADS - 1:
+                grp = before[0]
+                waiting.extend((grp, n, quad) for quad in range(QUADS) for n in range(GROUP_TILES[grp]))
+            transposed, waiting = waiting[:BANKS_PER_STEP], waiting[BANKS_PER_STEP:]
+            for item in transposed:
+                value_transpose(item)
+            if before and before[1] == QUADS - 1:
+                norm_root(before[0])
+            for chunk in turned:
+                x_copy(chunk)
+            copied = turned
+            s += 1

@@ -19,30 +19,21 @@ ACT = mybir.ActivationFunctionType
 
 P = 128
 TILES = T // P
-K_PASS = 512
+GROUP_TILES = 2
+GROUP = GROUP_TILES * P
+GROUPS = TILES // GROUP_TILES
+PACK = 4
+K_PASS = P * PACK
 PASSES = D // K_PASS
 BANK = 512
-QUAD = 4
+BANK_HEADS = BANK // GROUP
+QUAD = BANK // HD
 QUADS = HEADS // QUAD
-PAIR = 2
-GAIN_ROW = 32
-GROUP_TILES = (2, 2, 2, 1, 1)
-HEAD_CHUNKS = 4
-BANKS_PER_STEP = 2
-EARLY_STEPS = 3
-FOLD_STEPS = 2
-GADD = True
-ORDER = 0
-VT_BUFS = 3
-EARLY_HEADS = 4
-FOLD2 = False
-LATE_FROM = 5
-SCALES = 1
-XT = 1
-VADDS = 1
-SPLIT_FROM = 5
-SPLITS = 2
-TABLE_STEP = 2
+PAIRS = HD // 2
+ALIGN = 256
+
+PRODUCT_BANKS, TURN_BANKS, SUM_BANKS = 3, 4, 1
+TURNS, TURNS_AT_END = 2, 3
 
 
 def tile_causalwanmodel_pa_kernel(tc, x, w_words, w_scales, b, g, freqs_cos, freqs_sin, out):
@@ -56,72 +47,75 @@ def tile_causalwanmodel_pa_kernel(tc, x, w_words, w_scales, b, g, freqs_cos, fre
         psum = ctx.enter_context(tc.psum_pool(name="psum", bufs=1))
         ctx.enter_context(tc.manual_schedule())
 
-        rows_bf = keep.tile([P, P], BF16, name="rows_bf")
+        rows_bf = keep.tile([P, QUADS, HD], BF16, name="rows_bf")
         nc.vector.memset(rows_bf[:], 0.0)
         ident = keep.tile([P, P], F32, name="ident")
         make_identity(nc, ident[:])
+        ident_bf = keep.tile([P, P], BF16, name="ident_bf")
+        make_identity(nc, ident_bf[:])
 
-        x_raw = {}
+        x_raw, w_codes, w_plane = {}, {}, {}
 
         def load_x_pass(k):
-            t = keep.tile([P, PAIR, K_PASS], BF16, name="x_first%d" % k)
-            nc.sync.dma_start(out=t[:], in_=x_rows[:, 0:PAIR, K_PASS * k : K_PASS * (k + 1)])
+            t = keep.tile([P, GROUP_TILES, K_PASS], BF16, name="x_first%d" % k)
+            nc.sync.dma_start(out=t[:], in_=x_rows[:, 0:GROUP_TILES, K_PASS * k : K_PASS * (k + 1)])
             x_raw[0, k] = t[:]
 
-        def load_x_pair(pair):
-            t = keep.tile([P, PAIR, D], BF16, name="x_pair%d" % pair)
-            nc.sync.dma_start(out=t[:], in_=x_rows[:, PAIR * pair : PAIR * (pair + 1), :])
+        def load_x_group(grp):
+            t = keep.tile([P, GROUP_TILES, D], BF16, name="x_group%d" % grp)
+            nc.sync.dma_start(out=t[:], in_=x_rows[:, GROUP_TILES * grp : GROUP_TILES * (grp + 1), :])
             for k in range(PASSES):
-                x_raw[pair, k] = t[:, :, K_PASS * k : K_PASS * (k + 1)]
+                x_raw[grp, k] = t[:, :, K_PASS * k : K_PASS * (k + 1)]
 
-        w_codes = {}
-
-        def load_w(quad):
+        def load_codes(quad):
             width = 2 * QUAD * HD
-            t = keep.tile([P, PASSES, width], U8, name="w_codes%d" % quad, align_bytes=64)
+            t = keep.tile([P, PASSES, width], U8, name="w_codes%d" % quad, align_bytes=ALIGN)
             src = w_words[:, :, width * quad : width * (quad + 1)].rearrange("k p n -> p k n")
             nc.sync.dma_start(out=t[:].bitcast(I32), in_=src.bitcast(I32))
             w_codes[quad] = t
 
+        def load_scales(heads):
+            t = keep.tile([P, PASSES, HD * len(heads)], U8, name="w_plane%d" % heads[0], align_bytes=ALIGN)
+            for r in range(4):
+                src = w_scales[:, r:16:4, HD * heads[0] : HD * (heads[-1] + 1)].rearrange("k q n -> q k n")
+                nc.sync.dma_start(out=t[r:P:32, :, :].bitcast(I32), in_=src.bitcast(I32))
+            for i, head in enumerate(heads):
+                w_plane[head] = t[:, :, HD * i : HD * (i + 1)]
+
         for k in range(PASSES):
             load_x_pass(k)
-        w_plane = keep.tile([P, PASSES, D], U8, name="w_plane", align_bytes=64)
-        for q in range(4):
-            src = w_scales[:, 4 * q : 4 * q + 4, :].rearrange("k r n -> r k n")
-            nc.sync.dma_start(out=w_plane[32 * q : 32 * q + 4, :, :].bitcast(I32), in_=src.bitcast(I32))
-        load_w(0)
-        nc.sync.dma_start(out=rows_bf[0:HEADS, :], in_=b.rearrange("(h c) -> h c", c=HD))
-        nc.sync.dma_start(out=rows_bf[GAIN_ROW : GAIN_ROW + HEADS, :], in_=g.rearrange("(h c) -> h c", c=HD))
-        load_x_pair(1)
-        load_w(1)
-        load_w(2)
-        load_x_pair(2)
-        cos_bf = keep.tile([P, TILES * HD // 2], BF16, name="cos_bf")
-        sin_bf = keep.tile([P, TILES * HD // 2], BF16, name="sin_bf")
+        load_scales(range(QUAD))
+        load_codes(0)
+        nc.sync.dma_start(out=rows_bf[0:QUAD, :, :], in_=b.rearrange("(q i c) -> i q c", i=QUAD, c=HD))
+        nc.sync.dma_start(out=rows_bf[QUAD : 2 * QUAD, :, :], in_=g.rearrange("(q i c) -> i q c", i=QUAD, c=HD))
+        load_x_group(1)
+        load_scales(range(QUAD, HEADS))
+        load_codes(1)
+        load_codes(2)
+        load_x_group(2)
+        cos_bf = keep.tile([P, TILES * PAIRS], BF16, name="cos_bf")
+        sin_bf = keep.tile([P, TILES * PAIRS], BF16, name="sin_bf")
         nc.sync.dma_start(out=cos_bf[:], in_=freqs_cos.rearrange("(p n) j -> p (n j)", n=TILES))
         nc.sync.dma_start(out=sin_bf[:], in_=freqs_sin.rearrange("(p n) j -> p (n j)", n=TILES))
-        load_x_pair(3)
+        load_x_group(3)
 
-        x_codes, x_plane, x_banks, x_grouped = {}, {}, {}, {}
-
-        def x_transpose(chunk, tag, bufs):
-            bank = psum.tile([P, 2, PAIR, P], F32, name="x_bank", tag=tag, bufs=bufs)
-            for n in range(PAIR):
-                words = x_raw[chunk][:, n, :].bitcast(F32)
-                for u in range(2):
-                    src = x_split[chunk][:, n, u, :] if chunk in x_split else words[:, u : K_PASS // 2 : 2]
-                    nc.tensor.transpose(bank[:, u, n, :], src, ident[:])
-            x_banks[chunk] = bank
-
-        x_split = {}
+        chunks = [(grp, k) for grp in range(GROUPS) for k in range(PASSES)]
+        x_split, x_banks, x_grouped, x_codes, x_plane = {}, {}, {}, {}, {}
 
         def x_deinterleave(chunk):
-            t = keep.tile([P, PAIR, 2, P], F32, name="x_split%d_%d" % chunk)
+            t = keep.tile([P, GROUP_TILES, 2, P], F32, name="x_split%d_%d" % chunk)
             nc.vector.tensor_copy(out=t[:], in_=x_raw[chunk].bitcast(F32).rearrange("p n (m u) -> p n u m", u=2))
             x_split[chunk] = t
 
+        def x_transpose(chunk):
+            bank = psum.tile([P, 2, GROUP_TILES, P], F32, name="x_bank", tag="turn", bufs=TURN_BANKS)
+            for n in range(GROUP_TILES):
+                for u in range(2):
+                    nc.tensor.transpose(bank[:, u, n, :], x_split[chunk][:, n, u, :], ident[:])
+            x_banks[chunk] = bank
+
         def x_copy(chunk):
-            t = work.tile([P, PAIR * P * 4], BF16, name="x_grouped", align_bytes=64)
+            t = work.tile([P, GROUP * PACK], BF16, name="x_grouped", align_bytes=ALIGN)
             nc.scalar.copy(
                 out=t[:].bitcast(F32).rearrange("p (r u) -> p r u", u=2),
                 in_=x_banks[chunk][:].rearrange("p u n r -> p (n r) u"),
@@ -129,39 +123,34 @@ def tile_causalwanmodel_pa_kernel(tc, x, w_words, w_scales, b, g, freqs_cos, fre
             x_grouped[chunk] = t
 
         def x_quantize(chunk):
-            codes = keep.tile([P, PAIR * P], U32, name="x_codes%d_%d" % chunk, align_bytes=64)
-            plane = keep.tile([P, PAIR * P], U8, name="x_plane%d_%d" % chunk, align_bytes=64)
+            codes = keep.tile([P, GROUP], U32, name="x_codes%d_%d" % chunk, align_bytes=ALIGN)
+            plane = keep.tile([P, GROUP], U8, name="x_plane%d_%d" % chunk, align_bytes=ALIGN)
             nc.vector.quantize_mx(out=codes[:].bitcast(E5M2X4), scales=plane[:], in_=x_grouped[chunk][:])
             x_codes[chunk], x_plane[chunk] = codes, plane
 
-        chunks = [(pair, k) for pair in range(TILES // PAIR) for k in range(PASSES)]
-
         for chunk in chunks[:PASSES]:
-            x_transpose(chunk, "vt", VT_BUFS)
+            x_deinterleave(chunk)
+            x_transpose(chunk)
             x_copy(chunk)
-        for chunk in chunks[:2]:
-            x_quantize(chunk)
-        rows_f32 = keep.tile([P, P], F32, name="rows_f32")
-        nc.vector.tensor_copy(out=rows_f32[:], in_=rows_bf[:])
-        cols_bank = psum.tile([P, P], F32, name="cols_bank", tag="ss", bufs=1)
-        nc.tensor.transpose(cols_bank[:], rows_f32[:], ident[:])
-        for chunk in chunks[2:PASSES]:
-            x_quantize(chunk)
-        cols = keep.tile([P, 2 * GAIN_ROW], F32, name="cols")
-        nc.vector.tensor_copy(out=cols[:], in_=cols_bank[:, 0 : 2 * GAIN_ROW])
-        gain_bias = keep.tile([P, HEADS], F32, name="gain_bias")
-        nc.vector.tensor_tensor(
-            out=gain_bias[:], in0=cols[:, 0:HEADS], in1=cols[:, GAIN_ROW : GAIN_ROW + HEADS], op=ALU.mult
-        )
 
-        cos2 = keep.tile([P, TILES, HD // 2, 2], F32, name="cos2")
-        sin2 = keep.tile([P, TILES, HD // 2, 2], F32, name="sin2")
+        cols_bank = psum.tile([P, QUADS, P], BF16, name="cols_bank", tag="sum", bufs=SUM_BANKS)
+        for quad in range(QUADS):
+            nc.tensor.transpose(cols_bank[:, quad, :], rows_bf[:, quad, :], ident_bf[:])
+        for chunk in chunks[:PASSES]:
+            x_quantize(chunk)
+        cols = keep.tile([P, QUADS, 2 * QUAD], F32, name="cols")
+        nc.vector.tensor_copy(out=cols[:], in_=cols_bank[:, :, 0 : 2 * QUAD])
+        gain_bias = keep.tile([P, QUADS, QUAD], F32, name="gain_bias")
+        nc.vector.tensor_tensor(out=gain_bias[:], in0=cols[:, :, :QUAD], in1=cols[:, :, QUAD:], op=ALU.mult)
+
+        cos2 = keep.tile([P, TILES, PAIRS, 2], F32, name="cos2")
+        sin2 = keep.tile([P, TILES, PAIRS, 2], F32, name="sin2")
         sign = keep.tile([P, 1, 2], F32, name="sign")
         nc.vector.memset(sign[:, :, 0:1], -1.0)
         nc.vector.memset(sign[:, :, 1:2], 1.0)
 
-        def make_tables():
-            shape = [P, TILES * HD // 2, 2]
+        def make_factors():
+            shape = [P, TILES * PAIRS, 2]
             nc.scalar.copy(
                 out=cos2[:].rearrange("p n j e -> p (n j) e"),
                 in_=cos_bf[:].rearrange("p (m o) -> p m o", o=1).to_broadcast(shape),
@@ -173,214 +162,204 @@ def tile_causalwanmodel_pa_kernel(tc, x, w_words, w_scales, b, g, freqs_cos, fre
                 op=ALU.mult,
             )
 
-        first_tile = [sum(GROUP_TILES[:i]) for i in range(len(GROUP_TILES))]
-        steps = [(grp, quad) for grp in range(len(GROUP_TILES)) for quad in range(QUADS)]
-        mx_banks, gained, squares, folded, sum_bank, root, rstd, vt_banks = {}, {}, {}, {}, {}, {}, {}, {}
+        products, gained, squares, sum_bank, rstd, turned_banks = {}, {}, {}, {}, {}, {}
+        halves = [range(i, i + BANK_HEADS) for i in range(0, QUAD, BANK_HEADS)]
 
-        def multiply(step):
-            grp, quad = step
-            n = GROUP_TILES[grp] * P
-            pair, offset = divmod(first_tile[grp], PAIR)
-            tokens = slice(offset * P, offset * P + n)
-            per_bank = BANK // n
+        def multiply(grp, quad):
+            for half in halves:
+                bank = psum.tile([P, BANK_HEADS, GROUP], F32, name="product_bank", tag="product", bufs=PRODUCT_BANKS)
+                for j, i in enumerate(half):
+                    products[grp, quad, i] = bank[:, j, :]
             for i in range(QUAD):
-                if i % per_bank == 0:
-                    bank = psum.tile([P, per_bank, n], F32, name="mx_bank", tag="mx", bufs=7 - XT - VT_BUFS)
-                head = QUAD * quad + i
                 for k in range(PASSES):
                     nc.tensor.matmul_mx(
-                        out=bank[:, i % per_bank, :],
+                        out=products[grp, quad, i],
                         lhsT=w_codes[quad][:, k, 2 * HD * i : 2 * HD * (i + 1)].bitcast(E2M1X4),
-                        lhsT_scale=w_plane[:, k, HD * head : HD * (head + 1)],
-                        rhs=x_codes[pair, k][:, tokens].bitcast(E5M2X4),
-                        rhs_scale=x_plane[pair, k][:, tokens],
+                        lhsT_scale=w_plane[QUAD * quad + i][:, k, :],
+                        rhs=x_codes[grp, k][:].bitcast(E5M2X4),
+                        rhs_scale=x_plane[grp, k][:],
                         start=(k == 0),
                         stop=(k == PASSES - 1),
                     )
-                mx_banks[step, i] = bank[:, i % per_bank, :]
 
-        def evacuate(step, gain_on_vector):
-            grp, quad = step
-            n = GROUP_TILES[grp] * P
-            per_bank = BANK // n
-            squares[step] = work.tile([P, QUAD, n], F32, name="squares", bufs=2)
-            gained[step] = work.tile([P, QUAD, n], F32, name="gained", bufs=7)
-            for i0 in range(0, QUAD, per_bank):
-                for i in range(i0, i0 + per_bank):
-                    head = QUAD * quad + i
-                    nc.scalar.activation(
-                        out=squares[step][:, i, :],
-                        in_=mx_banks[step, i],
-                        func=ACT.Square,
-                        bias=cols[:, head : head + 1],
+        def square(grp, quad, half):
+            t = work.tile([P, BANK_HEADS, GROUP], F32, name="squares", bufs=6)
+            squares.setdefault((grp, quad), []).append(t)
+            for j, i in enumerate(half):
+                nc.scalar.activation(
+                    out=t[:, j, :], in_=products[grp, quad, i], func=ACT.Square, bias=cols[:, quad, i : i + 1]
+                )
+
+        def gain(grp, quad, half):
+            t = work.tile([P, BANK_HEADS, GROUP], F32, name="gained", bufs=12)
+            for j, i in enumerate(half):
+                gained[grp, quad, i] = t[:, j, :]
+                gain_col = cols[:, quad, QUAD + i : QUAD + i + 1]
+                bias_col = gain_bias[:, quad, i : i + 1]
+                if grp == 0:
+                    nc.vector.tensor_scalar(
+                        out=t[:, j, :],
+                        in0=products[grp, quad, i],
+                        scalar1=gain_col,
+                        scalar2=bias_col,
+                        op0=ALU.mult,
+                        op1=ALU.add,
                     )
-                for i in range(i0, i0 + per_bank):
-                    head = QUAD * quad + i
-                    gain = cols[:, GAIN_ROW + head : GAIN_ROW + head + 1]
-                    if i >= QUAD - gain_on_vector:
-                        nc.vector.tensor_scalar(
-                            out=gained[step][:, i, :],
-                            in0=mx_banks[step, i],
-                            scalar1=gain,
-                            scalar2=gain_bias[:, head : head + 1],
-                            op0=ALU.mult,
-                            op1=ALU.add,
-                        )
-                    else:
-                        nc.scalar.activation(
-                            out=gained[step][:, i, :],
-                            in_=mx_banks[step, i],
-                            func=ACT.Identity,
-                            bias=gain_bias[:, head : head + 1],
-                            scale=gain,
-                        )
+                else:
+                    nc.scalar.activation(
+                        out=t[:, j, :], in_=products[grp, quad, i], func=ACT.Identity, bias=bias_col, scale=gain_col
+                    )
 
-        def fold(step):
-            n = GROUP_TILES[step[0]] * P
-            if steps.index(step) >= FOLD_STEPS:
-                folded[step] = squares[step]
-                return
-            folded[step] = work.tile([P, QUAD // 2, n], F32, name="folded", bufs=2)
-            nc.vector.tensor_tensor(
-                out=folded[step][:],
-                in0=squares[step][:, : QUAD // 2, :],
-                in1=squares[step][:, QUAD // 2 :, :],
-                op=ALU.add,
-            )
-            if FOLD2:
-                twice = work.tile([P, 1, n], F32, name="twice", bufs=2)
-                nc.vector.tensor_tensor(out=twice[:], in0=folded[step][:, 0:1, :], in1=folded[step][:, 1:2, :], op=ALU.add)
-                folded[step] = twice
+        def evacuate(grp, quad):
+            if quad == QUADS - 1:
+                order = [(read, half) for read in (square, gain) for half in halves]
+            else:
+                order = [(read, half) for half in halves for read in (square, gain)]
+            for read, half in order:
+                read(grp, quad, half)
 
-        def sum_transpose(step):
-            grp, quad = step
-            tiles = GROUP_TILES[grp]
+        def fold(grp, quad):
+            first, second = squares[grp, quad]
+            t = work.tile([P, BANK_HEADS, GROUP], F32, name="folded", bufs=4)
+            nc.vector.tensor_tensor(out=t[:], in0=first[:], in1=second[:], op=ALU.add)
+            squares[grp, quad] = [t]
+
+        def sum_transpose(grp, quad):
             if quad == 0:
-                sum_bank[grp] = psum.tile([P, tiles, P], F32, name="sum_bank", tag="ss", bufs=1)
-            parts = [(i, n) for i in range(folded[step].shape[1]) for n in range(tiles)]
-            for i, n in parts:
+                sum_bank[grp] = psum.tile([P, GROUP_TILES, P], F32, name="sum_bank", tag="sum", bufs=SUM_BANKS)
+            parts = [(t, j, n) for t in squares[grp, quad] for j in range(BANK_HEADS) for n in range(GROUP_TILES)]
+            for i, (t, j, n) in enumerate(parts):
                 nc.tensor.matmul(
                     out=sum_bank[grp][:, n, :],
-                    lhsT=folded[step][:, i, P * n : P * (n + 1)],
+                    lhsT=t[:, j, P * n : P * (n + 1)],
                     rhs=ident[:],
-                    start=(quad == 0 and (i, n) == parts[0]),
-                    stop=(quad == QUADS - 1 and (i, n) == parts[-1]),
+                    start=(quad == 0 and i == 0),
+                    stop=(quad == QUADS - 1 and i == len(parts) - 1),
                     is_transpose=True,
                 )
 
-        def norm_root(grp):
-            tiles = GROUP_TILES[grp]
-            total = work.tile([P, tiles], F32, name="total")
-            for n in range(tiles):
-                spent = work.tile([P, P], F32, name="spent")
+        def norm_factor(grp):
+            total = work.tile([P, GROUP_TILES], F32, name="total")
+            for n in range(GROUP_TILES):
+                unread = work.tile([P, P], F32, name="unread")
                 nc.scalar.activation(
-                    out=spent[:], in_=sum_bank[grp][:, n, :], func=ACT.Identity, accum_out=total[:, n : n + 1]
+                    out=unread[:], in_=sum_bank[grp][:, n, :], func=ACT.Identity, accum_out=total[:, n : n + 1]
                 )
-            root[grp] = work.tile([P, tiles], F32, name="root")
-            nc.scalar.activation(
-                out=root[grp][:], in_=total[:], func=ACT.Abs_reciprocal_sqrt, bias=EPS, scale=1.0 / D
-            )
-
-        def norm_reciprocal(grp):
-            rstd[grp] = root[grp]
+            rstd[grp] = work.tile([P, GROUP_TILES], F32, name="rstd")
+            nc.scalar.activation(out=rstd[grp][:], in_=total[:], func=ACT.Abs_reciprocal_sqrt, bias=EPS, scale=1.0 / D)
 
         def value_transpose(item):
             grp, n, quad = item
-            bank = psum.tile([P, QUAD, HD // 2, 2], F32, name="vt_bank", tag="vt", bufs=VT_BUFS)
+            bank = psum.tile([P, QUAD, PAIRS, 2], F32, name="value_bank", tag="turn", bufs=TURN_BANKS)
             for i in range(QUAD):
                 nc.tensor.transpose(
                     bank[:, i, :, :].rearrange("p j e -> p (j e)"),
-                    gained[grp, quad][:, i, P * n : P * (n + 1)],
+                    gained[grp, quad, i][:, P * n : P * (n + 1)],
                     ident[:],
                 )
-            vt_banks[item] = bank
+            turned_banks[item] = bank
 
         def rotate(item):
             grp, n, quad = item
-            tile = first_tile[grp] + n
-            shape = [P, QUAD, HD // 2, 2]
-            bank = vt_banks[item]
-            by_cos = work.tile(shape, F32, name="by_cos")
-            by_sin = work.tile(shape, F32, name="by_sin")
-            for dst, src, table in ((by_cos, bank[:], cos2), (by_sin, bank[:, :, :, ::-1], sin2)):
+            tile = GROUP_TILES * grp + n
+            shape = [P, QUAD, PAIRS, 2]
+            bank = turned_banks[item]
+            by_cos = work.tile(shape, F32, name="by_cos", bufs=4)
+            by_sin = work.tile(shape, F32, name="by_sin", bufs=4)
+            for product, values, table in ((by_cos, bank[:], cos2), (by_sin, bank[:, :, :, ::-1], sin2)):
                 factor = table[:, tile : tile + 1, :, :].to_broadcast(shape)
                 if grp in rstd:
                     nc.vector.scalar_tensor_tensor(
-                        out=dst[:], in0=src, scalar=rstd[grp][:, n : n + 1], in1=factor, op0=ALU.mult, op1=ALU.mult
+                        out=product[:], in0=values, scalar=rstd[grp][:, n : n + 1], in1=factor, op0=ALU.mult, op1=ALU.mult
                     )
                 else:
-                    nc.vector.tensor_tensor(out=dst[:], in0=src, in1=factor, op=ALU.mult)
-            result = work.tile([P, BANK], F32, name="result", bufs=10)
-            adder = nc.vector if item in vector_adds or not GADD else nc.gpsimd
+                    nc.vector.tensor_tensor(out=product[:], in0=values, in1=factor, op=ALU.mult)
+            return item, by_cos, by_sin
+
+        def store(item, rows):
+            grp, n, quad = item
+            nc.sync.dma_start(out=out_rows[:, GROUP_TILES * grp + n, BANK * quad : BANK * (quad + 1)], in_=rows[:])
+
+        unscaled = []
+
+        def add_and_store(adder, item, by_cos, by_sin):
+            result = work.tile([P, BANK], F32, name="result", bufs=8)
             adder.tensor_tensor(
                 out=result[:],
                 in0=by_cos[:].rearrange("p i j e -> p (i j e)"),
                 in1=by_sin[:].rearrange("p i j e -> p (i j e)"),
                 op=ALU.add,
             )
-            if grp in rstd:
+            if item[0] in rstd:
                 store(item, result)
             else:
                 unscaled.append((item, result))
 
-        def store(item, result):
-            grp, n, quad = item
-            nc.sync.dma_start(out=out_rows[:, first_tile[grp] + n, BANK * quad : BANK * (quad + 1)], in_=result[:])
-
-        def scale_late(most):
-            for item, result in [entry for entry in unscaled if entry[0][0] in rstd][:most]:
-                grp, n, quad = item
-                unscaled.remove((item, result))
-                scaled = work.tile([P, BANK], F32, name="scaled", bufs=4)
+        def scale_and_store():
+            for (grp, n, quad), result in unscaled:
+                scaled = work.tile([P, BANK], F32, name="scaled", bufs=5)
                 nc.scalar.activation(out=scaled[:], in_=result[:], func=ACT.Copy, scale=rstd[grp][:, n : n + 1])
-                store(item, scaled)
+                store((grp, n, quad), scaled)
+            unscaled.clear()
 
-        unscaled = []
-        last_group = len(GROUP_TILES) - 1
-        vector_adds = [(last_group, n, QUADS - 1) for n in range(GROUP_TILES[last_group])][-VADDS:] if VADDS else []
-        copied = []
-        waiting = []
-        transposed = []
-        s = 0
-        while s <= len(steps) or waiting or transposed or unscaled:
-            step = steps[s] if s < len(steps) else None
-            before = steps[s - 1] if 1 <= s <= len(steps) else None
-            twice_before = steps[s - 2] if 2 <= s <= len(steps) + 1 else None
-            turned = chunks[PASSES + s + 1 : PASSES + s + 2] if s else chunks[PASSES : PASSES + 2]
-            if step:
-                multiply(step)
-            if before:
-                fold(before)
-            if twice_before and twice_before[1] == QUADS - 1:
-                norm_reciprocal(twice_before[0])
-            for item in transposed[:1]:
-                rotate(item)
+        steps = [(grp, quad) for grp in range(GROUPS) for quad in range(QUADS)]
+        items = [(grp, n, quad) for grp, quad in steps for n in range(GROUP_TILES)]
+        last = GROUPS - 1
+        folds = [steps[0]] + [(grp, 1) for grp in range(last)]
+        x_todo = chunks[PASSES:]
+        copied, turned = [], []
+
+        for s, (grp, quad) in enumerate(steps):
+            multiply(grp, quad)
+
+            port_work = [(fold, steps[s - 1])] if s and steps[s - 1] in folds else []
+            port_work += [(x_quantize, (chunk,)) for chunk in copied]
+            for item in turned:
+                rotated = rotate(item)
+                for call, args in port_work[:1]:
+                    call(*args)
+                port_work = port_work[1:]
+                add_and_store(nc.gpsimd, *rotated)
+            for call, args in port_work:
+                call(*args)
+
+            count = 2 if s == 0 else 1
+            copied, x_todo = x_todo[:count], x_todo[count:]
+            ahead = chunks[PASSES * (s + 1) : PASSES * (s + 2)] if grp == 0 else []
+            for chunk in ahead:
+                if chunk in copied:
+                    x_deinterleave(chunk)
+            evacuate(grp, quad)
+            if quad == 0:
+                scale_and_store()
+            for chunk in ahead:
+                if chunk not in copied:
+                    x_deinterleave(chunk)
+            if s == 1:
+                make_factors()
+
             for chunk in copied:
-                x_quantize(chunk)
-            for item in transposed[1:]:
-                rotate(item)
-            if step:
-                evacuate(step, EARLY_HEADS if s < EARLY_STEPS else 0)
-            scale_late(SCALES if step else 99)
-            for chunk in chunks[max(SPLIT_FROM, 2 * s + 4) : 2 * s + 6]:
-                x_deinterleave(chunk)
-            if s == TABLE_STEP:
-                make_tables()
-            if before:
-                sum_transpose(before)
-            for chunk in turned:
-                x_transpose(chunk, *(("xt", 1) if s and XT else ("vt", VT_BUFS)))
-            if before and before[0] >= LATE_FROM:
-                waiting.extend((before[0], n, before[1]) for n in range(GROUP_TILES[before[0]]))
-            elif before and before[1] == QUADS - 1:
-                grp = before[0]
-                waiting.extend((grp, n, quad) for quad in range(QUADS) for n in range(GROUP_TILES[grp]))
-            transposed, waiting = waiting[:BANKS_PER_STEP], waiting[BANKS_PER_STEP:]
-            for item in transposed:
+                x_transpose(chunk)
+            count = 0 if s < QUADS - 1 else TURNS_AT_END if grp == last and quad < QUADS - 1 else TURNS
+            turned, items = items[:count], items[count:]
+            for item in turned:
                 value_transpose(item)
-            if before and before[1] == QUADS - 1:
-                norm_root(before[0])
-            for chunk in turned:
+            if quad > 0:
+                sum_transpose(grp, quad - 1)
+            if quad == QUADS - 1:
+                sum_transpose(grp, quad)
+                if grp == last - 1:
+                    add_and_store(nc.gpsimd, *rotate(turned[0]))
+                    turned = turned[1:]
+                if grp == last:
+                    add_and_store(nc.vector, *rotate(turned[0]))
+                    add_and_store(nc.gpsimd, *rotate(turned[1]))
+                norm_factor(grp)
+            for chunk in copied:
                 x_copy(chunk)
-            copied = turned
-            s += 1
+
+        scale_and_store()
+        for item in items:
+            value_transpose(item)
+        for rotated in [rotate(item) for item in items]:
+            add_and_store(nc.vector, *rotated)

@@ -86,9 +86,9 @@ def tile_causalwanmodel_pa_kernel(tc, x, w_words, w_scales, b, g, freqs_cos, fre
             load_x_pass(k)
         load_scales(range(QUAD))
         load_codes(0)
+        load_x_group(1)
         nc.sync.dma_start(out=rows_bf[0:QUAD, :, :], in_=b.rearrange("(q i c) -> i q c", i=QUAD, c=HD))
         nc.sync.dma_start(out=rows_bf[QUAD : 2 * QUAD, :, :], in_=g.rearrange("(q i c) -> i q c", i=QUAD, c=HD))
-        load_x_group(1)
         load_scales(range(QUAD, HEADS))
         load_codes(1)
         load_codes(2)
@@ -133,15 +133,18 @@ def tile_causalwanmodel_pa_kernel(tc, x, w_words, w_scales, b, g, freqs_cos, fre
             x_transpose(chunk)
             x_copy(chunk)
 
-        cols_bank = psum.tile([P, QUADS, P], BF16, name="cols_bank", tag="sum", bufs=SUM_BANKS)
-        for quad in range(QUADS):
-            nc.tensor.transpose(cols_bank[:, quad, :], rows_bf[:, quad, :], ident_bf[:])
         for chunk in chunks[:PASSES]:
             x_quantize(chunk)
+
         cols = keep.tile([P, QUADS, 2 * QUAD], F32, name="cols")
-        nc.vector.tensor_copy(out=cols[:], in_=cols_bank[:, :, 0 : 2 * QUAD])
         gain_bias = keep.tile([P, QUADS, QUAD], F32, name="gain_bias")
-        nc.vector.tensor_tensor(out=gain_bias[:], in0=cols[:, :, :QUAD], in1=cols[:, :, QUAD:], op=ALU.mult)
+
+        def make_columns():
+            bank = psum.tile([P, QUADS, P], BF16, name="cols_bank", tag="sum", bufs=SUM_BANKS)
+            for quad in range(QUADS):
+                nc.tensor.transpose(bank[:, quad, :], rows_bf[:, quad, :], ident_bf[:])
+            nc.vector.tensor_copy(out=cols[:], in_=bank[:, :, 0 : 2 * QUAD])
+            nc.vector.tensor_tensor(out=gain_bias[:], in0=cols[:, :, :QUAD], in1=cols[:, :, QUAD:], op=ALU.mult)
 
         cos2 = keep.tile([P, TILES, PAIRS, 2], F32, name="cos2")
         sin2 = keep.tile([P, TILES, PAIRS, 2], F32, name="sin2")
@@ -170,17 +173,27 @@ def tile_causalwanmodel_pa_kernel(tc, x, w_words, w_scales, b, g, freqs_cos, fre
                 bank = psum.tile([P, BANK_HEADS, GROUP], F32, name="product_bank", tag="product", bufs=PRODUCT_BANKS)
                 for j, i in enumerate(half):
                     products[grp, quad, i] = bank[:, j, :]
-            for i in range(QUAD):
-                for k in range(PASSES):
-                    nc.tensor.matmul_mx(
-                        out=products[grp, quad, i],
-                        lhsT=w_codes[quad][:, k, 2 * HD * i : 2 * HD * (i + 1)].bitcast(E2M1X4),
-                        lhsT_scale=w_plane[QUAD * quad + i][:, k, :],
-                        rhs=x_codes[grp, k][:].bitcast(E5M2X4),
-                        rhs_scale=x_plane[grp, k][:],
-                        start=(k == 0),
-                        stop=(k == PASSES - 1),
-                    )
+            if (grp, quad) == (0, 0):
+                order = [
+                    (i, k, k == 0 and i == half[0], k == PASSES - 1 and i == half[-1])
+                    for k in range(PASSES)
+                    for half in halves
+                    for i in half
+                ]
+            else:
+                order = [(i, k, k == 0, k == PASSES - 1) for i in range(QUAD) for k in range(PASSES)]
+            for i, k, start, stop in order:
+                if (grp, quad, k, i) == (0, 0, PASSES - 1, 0):
+                    make_columns()
+                nc.tensor.matmul_mx(
+                    out=products[grp, quad, i],
+                    lhsT=w_codes[quad][:, k, 2 * HD * i : 2 * HD * (i + 1)].bitcast(E2M1X4),
+                    lhsT_scale=w_plane[QUAD * quad + i][:, k, :],
+                    rhs=x_codes[grp, k][:].bitcast(E5M2X4),
+                    rhs_scale=x_plane[grp, k][:],
+                    start=start,
+                    stop=stop,
+                )
 
         def square(grp, quad, half):
             t = work.tile([P, BANK_HEADS, GROUP], F32, name="squares", bufs=6)
@@ -191,12 +204,13 @@ def tile_causalwanmodel_pa_kernel(tc, x, w_words, w_scales, b, g, freqs_cos, fre
                 )
 
         def gain(grp, quad, half):
+            on_vector = grp == 0 and (quad < QUADS - 1 or half == halves[-1])
             t = work.tile([P, BANK_HEADS, GROUP], F32, name="gained", bufs=12)
             for j, i in enumerate(half):
                 gained[grp, quad, i] = t[:, j, :]
                 gain_col = cols[:, quad, QUAD + i : QUAD + i + 1]
                 bias_col = gain_bias[:, quad, i : i + 1]
-                if grp == 0:
+                if on_vector:
                     nc.vector.tensor_scalar(
                         out=t[:, j, :],
                         in0=products[grp, quad, i],
@@ -309,6 +323,9 @@ def tile_causalwanmodel_pa_kernel(tc, x, w_words, w_scales, b, g, freqs_cos, fre
         x_todo = chunks[PASSES:]
         copied, turned = [], []
 
+        for k in range(PASSES):
+            x_deinterleave((1, k))
+
         for s, (grp, quad) in enumerate(steps):
             multiply(grp, quad)
 
@@ -325,17 +342,13 @@ def tile_causalwanmodel_pa_kernel(tc, x, w_words, w_scales, b, g, freqs_cos, fre
 
             count = 2 if s == 0 else 1
             copied, x_todo = x_todo[:count], x_todo[count:]
-            ahead = chunks[PASSES * (s + 1) : PASSES * (s + 2)] if grp == 0 else []
-            for chunk in ahead:
-                if chunk in copied:
-                    x_deinterleave(chunk)
             evacuate(grp, quad)
             if quad == 0:
                 scale_and_store()
-            for chunk in ahead:
-                if chunk not in copied:
-                    x_deinterleave(chunk)
-            if s == 1:
+            if grp == 0 and quad > 0:
+                for k in range(PASSES):
+                    x_deinterleave((quad + 1, k))
+            if s == QUADS - 1:
                 make_factors()
 
             for chunk in copied:
@@ -352,8 +365,9 @@ def tile_causalwanmodel_pa_kernel(tc, x, w_words, w_scales, b, g, freqs_cos, fre
                     add_and_store(nc.gpsimd, *rotate(turned[0]))
                     turned = turned[1:]
                 if grp == last:
-                    add_and_store(nc.vector, *rotate(turned[0]))
-                    add_and_store(nc.gpsimd, *rotate(turned[1]))
+                    first, second = [rotate(item) for item in turned]
+                    add_and_store(nc.vector, *first)
+                    add_and_store(nc.gpsimd, *second)
                 norm_factor(grp)
             for chunk in copied:
                 x_copy(chunk)

from contextlib import ExitStack

import concourse.mybir as mybir
from concourse.masks import make_identity

T, D, HEADS, HD = 1024, 1536, 12, 128
EPS = 1e-6
FLOPS = 2 * T * D * D

F32 = mybir.dt.float32
BF16 = mybir.dt.bfloat16
I32 = mybir.dt.int32
U32 = mybir.dt.uint32
U8 = mybir.dt.uint8
E5M2X4 = mybir.dt.float8_e5m2_x4
E2M1X4 = mybir.dt.float4_e2m1fn_x4
ALU = mybir.AluOpType
ACT = mybir.ActivationFunctionType

P = 128
TILES = T // P
GROUP_TILES = 2
GROUP = GROUP_TILES * P
GROUPS = TILES // GROUP_TILES
PACK = 4
K_PASS = P * PACK
PASSES = D // K_PASS
BANK = 512
BANK_HEADS = BANK // GROUP
QUAD = BANK // HD
QUADS = HEADS // QUAD
PAIRS = HD // 2
ALIGN = 256

PRODUCT_BANKS, TURN_BANKS, SUM_BANKS = 3, 4, 1
TURNS, TURNS_AT_END = 2, 3


def tile_causalwanmodel_pa_kernel(tc, x, w_words, w_scales, b, g, freqs_cos, freqs_sin, out):
    nc = tc.nc
    x_rows = x.rearrange("o (p n) d -> p (o n) d", n=TILES)
    out_rows = out.rearrange("o (p n) h c -> p (o n) (h c)", n=TILES)

    with ExitStack() as ctx:
        keep = ctx.enter_context(tc.tile_pool(name="keep", bufs=1))
        work = ctx.enter_context(tc.tile_pool(name="work", bufs=3))
        psum = ctx.enter_context(tc.psum_pool(name="psum", bufs=1))
        ctx.enter_context(tc.manual_schedule())

        rows_bf = keep.tile([P, QUADS, HD], BF16, name="rows_bf")
        nc.vector.memset(rows_bf[:], 0.0)
        ident = keep.tile([P, P], F32, name="ident")
        make_identity(nc, ident[:])
        ident_bf = keep.tile([P, P], BF16, name="ident_bf")
        make_identity(nc, ident_bf[:])

        x_raw, w_codes, w_plane = {}, {}, {}

        def load_x_pass(k):
            t = keep.tile([P, GROUP_TILES, K_PASS], BF16, name="x_first%d" % k)
            nc.sync.dma_start(out=t[:], in_=x_rows[:, 0:GROUP_TILES, K_PASS * k : K_PASS * (k + 1)])
            x_raw[0, k] = t[:]

        def load_x_group(grp):
            t = keep.tile([P, GROUP_TILES, D], BF16, name="x_group%d" % grp)
            nc.sync.dma_start(out=t[:], in_=x_rows[:, GROUP_TILES * grp : GROUP_TILES * (grp + 1), :])
            for k in range(PASSES):
                x_raw[grp, k] = t[:, :, K_PASS * k : K_PASS * (k + 1)]

        def load_codes(quad):
            width = 2 * QUAD * HD
            t = keep.tile([P, PASSES, width], U8, name="w_codes%d" % quad, align_bytes=ALIGN)
            src = w_words[:, :, width * quad : width * (quad + 1)].rearrange("k p n -> p k n")
            nc.sync.dma_start(out=t[:].bitcast(I32), in_=src.bitcast(I32))
            w_codes[quad] = t

        def load_scales(heads):
            t = keep.tile([P, PASSES, HD * len(heads)], U8, name="w_plane%d" % heads[0], align_bytes=ALIGN)
            for r in range(4):
                src = w_scales[:, r:16:4, HD * heads[0] : HD * (heads[-1] + 1)].rearrange("k q n -> q k n")
                nc.sync.dma_start(out=t[r:P:32, :, :].bitcast(I32), in_=src.bitcast(I32))
            for i, head in enumerate(heads):
                w_plane[head] = t[:, :, HD * i : HD * (i + 1)]

        for k in range(PASSES):
            load_x_pass(k)
        load_scales(range(QUAD))
        load_codes(0)
        load_x_group(1)
        nc.sync.dma_start(out=rows_bf[0:QUAD, :, :], in_=b.rearrange("(q i c) -> i q c", i=QUAD, c=HD))
        nc.sync.dma_start(out=rows_bf[QUAD : 2 * QUAD, :, :], in_=g.rearrange("(q i c) -> i q c", i=QUAD, c=HD))
        load_scales(range(QUAD, HEADS))
        load_codes(1)
        load_codes(2)
        load_x_group(2)
        cos_bf = keep.tile([P, TILES * PAIRS], BF16, name="cos_bf")
        sin_bf = keep.tile([P, TILES * PAIRS], BF16, name="sin_bf")
        nc.sync.dma_start(out=cos_bf[:], in_=freqs_cos.rearrange("(p n) j -> p (n j)", n=TILES))
        nc.sync.dma_start(out=sin_bf[:], in_=freqs_sin.rearrange("(p n) j -> p (n j)", n=TILES))
        load_x_group(3)

        chunks = [(grp, k) for grp in range(GROUPS) for k in range(PASSES)]
        x_split, x_banks, x_grouped, x_codes, x_plane = {}, {}, {}, {}, {}

        def x_deinterleave(chunk):
            t = keep.tile([P, GROUP_TILES, 2, P], F32, name="x_split%d_%d" % chunk)
            nc.vector.tensor_copy(out=t[:], in_=x_raw[chunk].bitcast(F32).rearrange("p n (m u) -> p n u m", u=2))
            x_split[chunk] = t

        def x_transpose(chunk):
            bank = psum.tile([P, 2, GROUP_TILES, P], F32, name="x_bank", tag="turn", bufs=TURN_BANKS)
            for n in range(GROUP_TILES):
                for u in range(2):
                    nc.tensor.transpose(bank[:, u, n, :], x_split[chunk][:, n, u, :], ident[:])
            x_banks[chunk] = bank

        def x_copy(chunk):
            t = work.tile([P, GROUP * PACK], BF16, name="x_grouped", align_bytes=ALIGN)
            nc.scalar.copy(
                out=t[:].bitcast(F32).rearrange("p (r u) -> p r u", u=2),
                in_=x_banks[chunk][:].rearrange("p u n r -> p (n r) u"),
            )
            x_grouped[chunk] = t

        def x_quantize(chunk):
            codes = keep.tile([P, GROUP], U32, name="x_codes%d_%d" % chunk, align_bytes=ALIGN)
            plane = keep.tile([P, GROUP], U8, name="x_plane%d_%d" % chunk, align_bytes=ALIGN)
            nc.vector.quantize_mx(out=codes[:].bitcast(E5M2X4), scales=plane[:], in_=x_grouped[chunk][:])
            x_codes[chunk], x_plane[chunk] = codes, plane

        for chunk in chunks[:PASSES]:
            x_deinterleave(chunk)
            x_transpose(chunk)
            x_copy(chunk)

        for chunk in chunks[:PASSES]:
            x_quantize(chunk)

        cols = keep.tile([P, QUADS, 2 * QUAD], F32, name="cols")
        gain_bias = keep.tile([P, QUADS, QUAD], F32, name="gain_bias")

        def make_columns():
            bank = psum.tile([P, QUADS, P], BF16, name="cols_bank", tag="sum", bufs=SUM_BANKS)
            for quad in range(QUADS):
                nc.tensor.transpose(bank[:, quad, :], rows_bf[:, quad, :], ident_bf[:])
            nc.vector.tensor_copy(out=cols[:], in_=bank[:, :, 0 : 2 * QUAD])
            nc.vector.tensor_tensor(out=gain_bias[:], in0=cols[:, :, :QUAD], in1=cols[:, :, QUAD:], op=ALU.mult)

        cos2 = keep.tile([P, TILES, PAIRS, 2], F32, name="cos2")
        sin2 = keep.tile([P, TILES, PAIRS, 2], F32, name="sin2")
        sign = keep.tile([P, 1, 2], F32, name="sign")
        nc.vector.memset(sign[:, :, 0:1], -1.0)
        nc.vector.memset(sign[:, :, 1:2], 1.0)

        def make_factors():
            shape = [P, TILES * PAIRS, 2]
            nc.scalar.copy(
                out=cos2[:].rearrange("p n j e -> p (n j) e"),
                in_=cos_bf[:].rearrange("p (m o) -> p m o", o=1).to_broadcast(shape),
            )
            nc.vector.tensor_tensor(
                out=sin2[:].rearrange("p n j e -> p (n j) e"),
                in0=sin_bf[:].rearrange("p (m o) -> p m o", o=1).to_broadcast(shape),
                in1=sign[:].to_broadcast(shape),
                op=ALU.mult,
            )

        products, gained, squares, sum_bank, rstd, turned_banks = {}, {}, {}, {}, {}, {}
        halves = [range(i, i + BANK_HEADS) for i in range(0, QUAD, BANK_HEADS)]

        def multiply(grp, quad):
            for half in halves:
                bank = psum.tile([P, BANK_HEADS, GROUP], F32, name="product_bank", tag="product", bufs=PRODUCT_BANKS)
                for j, i in enumerate(half):
                    products[grp, quad, i] = bank[:, j, :]
            if (grp, quad) == (0, 0):
                order = [
                    (i, k, k == 0 and i == half[0], k == PASSES - 1 and i == half[-1])
                    for k in range(PASSES)
                    for half in halves
                    for i in half
                ]
            else:
                order = [(i, k, k == 0, k == PASSES - 1) for i in range(QUAD) for k in range(PASSES)]
            for i, k, start, stop in order:
                if (grp, quad, k, i) == (0, 0, PASSES - 1, 0):
                    make_columns()
                nc.tensor.matmul_mx(
                    out=products[grp, quad, i],
                    lhsT=w_codes[quad][:, k, 2 * HD * i : 2 * HD * (i + 1)].bitcast(E2M1X4),
                    lhsT_scale=w_plane[QUAD * quad + i][:, k, :],
                    rhs=x_codes[grp, k][:].bitcast(E5M2X4),
                    rhs_scale=x_plane[grp, k][:],
                    start=start,
                    stop=stop,
                )

        def square(grp, quad, half):
            t = work.tile([P, BANK_HEADS, GROUP], F32, name="squares", bufs=6)
            squares.setdefault((grp, quad), []).append(t)
            for j, i in enumerate(half):
                nc.scalar.activation(
                    out=t[:, j, :], in_=products[grp, quad, i], func=ACT.Square, bias=cols[:, quad, i : i + 1]
                )

        def gain(grp, quad, half):
            on_vector = grp == 0 and (quad < QUADS - 1 or half == halves[-1])
            t = work.tile([P, BANK_HEADS, GROUP], F32, name="gained", bufs=12)
            for j, i in enumerate(half):
                gained[grp, quad, i] = t[:, j, :]
                gain_col = cols[:, quad, QUAD + i : QUAD + i + 1]
                bias_col = gain_bias[:, quad, i : i + 1]
                if on_vector:
                    nc.vector.tensor_scalar(
                        out=t[:, j, :],
                        in0=products[grp, quad, i],
                        scalar1=gain_col,
                        scalar2=bias_col,
                        op0=ALU.mult,
                        op1=ALU.add,
                    )
                else:
                    nc.scalar.activation(
                        out=t[:, j, :], in_=products[grp, quad, i], func=ACT.Identity, bias=bias_col, scale=gain_col
                    )

        def evacuate(grp, quad):
            if quad == QUADS - 1:
                order = [(read, half) for read in (square, gain) for half in halves]
            else:
                order = [(read, half) for half in halves for read in (square, gain)]
            for read, half in order:
                read(grp, quad, half)

        def fold(grp, quad):
            first, second = squares[grp, quad]
            t = work.tile([P, BANK_HEADS, GROUP], F32, name="folded", bufs=4)
            nc.vector.tensor_tensor(out=t[:], in0=first[:], in1=second[:], op=ALU.add)
            squares[grp, quad] = [t]

        def sum_transpose(grp, quad):
            if quad == 0:
                sum_bank[grp] = psum.tile([P, GROUP_TILES, P], F32, name="sum_bank", tag="sum", bufs=SUM_BANKS)
            parts = [(t, j, n) for t in squares[grp, quad] for j in range(BANK_HEADS) for n in range(GROUP_TILES)]
            for i, (t, j, n) in enumerate(parts):
                nc.tensor.matmul(
                    out=sum_bank[grp][:, n, :],
                    lhsT=t[:, j, P * n : P * (n + 1)],
                    rhs=ident[:],
                    start=(quad == 0 and i == 0),
                    stop=(quad == QUADS - 1 and i == len(parts) - 1),
                    is_transpose=True,
                )

        def norm_factor(grp):
            total = work.tile([P, GROUP_TILES], F32, name="total")
            for n in range(GROUP_TILES):
                unread = work.tile([P, P], F32, name="unread")
                nc.scalar.activation(
                    out=unread[:], in_=sum_bank[grp][:, n, :], func=ACT.Identity, accum_out=total[:, n : n + 1]
                )
            rstd[grp] = work.tile([P, GROUP_TILES], F32, name="rstd")
            nc.scalar.activation(out=rstd[grp][:], in_=total[:], func=ACT.Abs_reciprocal_sqrt, bias=EPS, scale=1.0 / D)

        def value_transpose(item):
            grp, n, quad = item
            bank = psum.tile([P, QUAD, PAIRS, 2], F32, name="value_bank", tag="turn", bufs=TURN_BANKS)
            for i in range(QUAD):
                nc.tensor.transpose(
                    bank[:, i, :, :].rearrange("p j e -> p (j e)"),
                    gained[grp, quad, i][:, P * n : P * (n + 1)],
                    ident[:],
                )
            turned_banks[item] = bank

        def rotate(item):
            grp, n, quad = item
            tile = GROUP_TILES * grp + n
            shape = [P, QUAD, PAIRS, 2]
            bank = turned_banks[item]
            by_cos = work.tile(shape, F32, name="by_cos", bufs=4)
            by_sin = work.tile(shape, F32, name="by_sin", bufs=4)
            for product, values, table in ((by_cos, bank[:], cos2), (by_sin, bank[:, :, :, ::-1], sin2)):
                factor = table[:, tile : tile + 1, :, :].to_broadcast(shape)
                if grp in rstd:
                    nc.vector.scalar_tensor_tensor(
                        out=product[:], in0=values, scalar=rstd[grp][:, n : n + 1], in1=factor, op0=ALU.mult, op1=ALU.mult
                    )
                else:
                    nc.vector.tensor_tensor(out=product[:], in0=values, in1=factor, op=ALU.mult)
            return item, by_cos, by_sin

        def store(item, rows):
            grp, n, quad = item
            nc.sync.dma_start(out=out_rows[:, GROUP_TILES * grp + n, BANK * quad : BANK * (quad + 1)], in_=rows[:])

        unscaled = []

        def add_and_store(adder, item, by_cos, by_sin):
            result = work.tile([P, BANK], F32, name="result", bufs=8)
            adder.tensor_tensor(
                out=result[:],
                in0=by_cos[:].rearrange("p i j e -> p (i j e)"),
                in1=by_sin[:].rearrange("p i j e -> p (i j e)"),
                op=ALU.add,
            )
            if item[0] in rstd:
                store(item, result)
            else:
                unscaled.append((item, result))

        def scale_and_store():
            for (grp, n, quad), result in unscaled:
                scaled = work.tile([P, BANK], F32, name="scaled", bufs=5)
                nc.scalar.activation(out=scaled[:], in_=result[:], func=ACT.Copy, scale=rstd[grp][:, n : n + 1])
                store((grp, n, quad), scaled)
            unscaled.clear()

        steps = [(grp, quad) for grp in range(GROUPS) for quad in range(QUADS)]
        items = [(grp, n, quad) for grp, quad in steps for n in range(GROUP_TILES)]
        last = GROUPS - 1
        folds = [steps[0]] + [(grp, 1) for grp in range(last)]
        x_todo = chunks[PASSES:]
        copied, turned = [], []

        for k in range(PASSES):
            x_deinterleave((1, k))

        for s, (grp, quad) in enumerate(steps):
            multiply(grp, quad)

            port_work = [(fold, steps[s - 1])] if s and steps[s - 1] in folds else []
            port_work += [(x_quantize, (chunk,)) for chunk in copied]
            for item in turned:
                rotated = rotate(item)
                for call, args in port_work[:1]:
                    call(*args)
                port_work = port_work[1:]
                add_and_store(nc.gpsimd, *rotated)
            for call, args in port_work:
                call(*args)

            count = 2 if s == 0 else 1
            copied, x_todo = x_todo[:count], x_todo[count:]
            evacuate(grp, quad)
            if quad == 0:
                scale_and_store()
            if grp == 0 and quad > 0:
                for k in range(PASSES):
                    x_deinterleave((quad + 1, k))
            if s == QUADS - 1:
                make_factors()

            for chunk in copied:
                x_transpose(chunk)
            count = 0 if s < QUADS - 1 else TURNS_AT_END if grp == last and quad < QUADS - 1 else TURNS
            turned, items = items[:count], items[count:]
            for item in turned:
                value_transpose(item)
            if quad > 0:
                sum_transpose(grp, quad - 1)
            if quad == QUADS - 1:
                sum_transpose(grp, quad)
                if grp == last - 1:
                    add_and_store(nc.gpsimd, *rotate(turned[0]))
                    turned = turned[1:]
                if grp == last:
                    first, second = [rotate(item) for item in turned]
                    add_and_store(nc.vector, *first)
                    add_and_store(nc.gpsimd, *second)
                norm_factor(grp)
            for chunk in copied:
                x_copy(chunk)

        scale_and_store()
        for item in items:
            value_transpose(item)
        for rotated in [rotate(item) for item in items]:
            add_and_store(nc.vector, *rotated)
